import numpy as np
import ml_dtypes


def mxq(x, axis, fmt="e4m3"):
    dtype, down = {"e4m3": (ml_dtypes.float8_e4m3fn, 7), "e5m2": (ml_dtypes.float8_e5m2, 14)}[fmt]
    v = np.moveaxis(np.asarray(x, np.float32).astype(ml_dtypes.bfloat16).astype(np.float64), axis, -1)
    blocks = v.reshape(v.shape[:-1] + (-1, 32))
    amax = np.abs(blocks).max(-1, keepdims=True)
    byte = np.maximum(np.where(amax > 0, np.frexp(amax)[1] - 1 + 127, 0) - down, 1)
    scale = np.exp2(byte - 127.0)
    codes = (blocks / scale).astype(np.float32).astype(dtype).astype(np.float64)
    return np.moveaxis((codes * scale).reshape(v.shape), -1, axis)


WIDE = False


def mx_kscale(k):
    if not WIDE:
        return np.ones(k)
    levels = np.array([10, -10, 5, -5, 0])
    a = np.random.permutation(np.resize(levels, k // 512 * 4)).reshape(k // 512, 4)
    idx = np.arange(k)
    return np.exp2(a[idx // 512, idx % 128 // 32])


BF16 = ml_dtypes.bfloat16


def bf(x):
    return np.asarray(x, np.float32).astype(BF16)


def f64(x):
    return np.asarray(x).astype(np.float64)


B, S, W, QK, E, V, H = 1, 1024, 1024, 128, 2048, 1024, 1
N = 2 * QK + 2 * E


def erf(v):
    a = np.clip(v, -6.0, 6.0)
    a2 = a * a
    term = a.copy()
    tot = a.copy()
    for n in range(1, 100):
        term = term * (a2 / (n + 0.5))
        tot = tot + term
    return 2.0 / np.sqrt(np.pi) * np.exp(-a2) * tot


def gelu_erf(v):
    return 0.5 * v * (1.0 + erf(v / np.sqrt(2.0)))


def setup_inputs():
    s = mx_kscale(W)
    g = np.where(np.arange(N) < 2 * QK, 1.4, 1.0)
    return {"x": bf(np.random.standard_normal((B, S, W)) * 1.5 + 0.5),
            "norm_w": bf((1.0 + 0.1 * np.random.standard_normal(W)) * s),
            "expand_w": bf(np.random.standard_normal((N, W)) * g[:, None] / np.sqrt(W) / s[None, :])}


def reference(x, norm_w, expand_w):
    x = f64(x)
    mu = x.mean(-1, keepdims=True)
    var = x.var(-1, keepdims=True)
    xn = (x - mu) / np.sqrt(var + 1e-5) * f64(norm_w)
    hidden = mxq(xn, 2, "e4m3") @ mxq(f64(expand_w), 1, "e4m3").T
    q = hidden[..., :QK]
    k = hidden[..., QK:2 * QK]
    lin = hidden[..., 2 * QK:2 * QK + E]
    pre = hidden[..., 2 * QK + E:]
    geglu = lin * gelu_erf(pre)
    return q, k, geglu

@@ -1,0 +1,297 @@
+from contextlib import ExitStack
+
+import concourse.masks as masks
+import concourse.mybir as mybir
+
+F32 = mybir.dt.float32
+BF16 = mybir.dt.bfloat16
+U32 = mybir.dt.uint32
+U8 = mybir.dt.uint8
+FP8X4 = mybir.dt.float8_e4m3fn_x4
+ACT = mybir.ActivationFunctionType
+ALU = mybir.AluOpType
+
+P = 128
+PACK = 4
+K = 1024
+PASSES = K // (P * PACK)
+WORDS = K // 2
+ROWS = 1024
+N_BLOCKS = ROWS // P
+QK = 256
+E = 2048
+CHUNK = 512
+CHUNK_ROW_BLOCKS = CHUNK // P
+N_PAIRS = E // CHUNK
+PRE, LIN = 0, 1
+N_ROW_BLOCKS = (QK + 2 * E) // P
+EPS = 1e-5
+FIRST_BLOCKS = 2
+W_BANKS_ON_VECTOR = 1
+
+FLOPS = 2 * ROWS * K * (QK + 2 * E)
+
+
+def tile_latentattentionblock_pa_kernel(tc, x, norm_w, expand_w, out_0, out_1, out_2):
+    nc = tc.nc
+    with ExitStack() as ctx:
+        ctx.enter_context(tc.manual_schedule())
+        resident = ctx.enter_context(tc.tile_pool(name="resident", bufs=1))
+        small = ctx.enter_context(tc.tile_pool(name="small", bufs=3))
+        staging = ctx.enter_context(tc.tile_pool(name="staging", bufs=2))
+        gated = ctx.enter_context(tc.tile_pool(name="gated", bufs=3))
+        results = ctx.enter_context(tc.tile_pool(name="results", bufs=12))
+        work_banks = ctx.enter_context(tc.psum_pool(name="work_banks", bufs=3))
+        pre_banks = ctx.enter_context(tc.psum_pool(name="pre_banks", bufs=2))
+        lin_banks = ctx.enter_context(tc.psum_pool(name="lin_banks", bufs=3))
+
+        x_rows = x.rearrange("o (p i) w -> p (o i) w", i=N_BLOCKS)
+        q_rows = out_0.rearrange("o (p i) d -> p (o i) d", i=N_BLOCKS)
+        k_rows = out_1.rearrange("o (p i) d -> p (o i) d", i=N_BLOCKS)
+        geglu_rows = out_2.rearrange("o (p i) d -> p (o i) d", i=N_BLOCKS)
+
+        x_raw = resident.tile([P, N_BLOCKS, K], BF16, name="x_raw")
+        w_raw = resident.tile([P, N_ROW_BLOCKS * K], BF16, name="w_raw")
+        w_words = w_raw[:].bitcast(F32)
+        x_codes = resident.tile([P, N_BLOCKS * PASSES * P], U32, name="x_codes", align_bytes=64)
+        x_scales = resident.tile([P, N_BLOCKS * PASSES * P], U8, name="x_scales", align_bytes=64)
+        w_codes = resident.tile([P, 2 * N_PAIRS * PASSES * CHUNK], U32, name="w_codes", align_bytes=64)
+        w_scales = resident.tile([P, 2 * N_PAIRS * PASSES * CHUNK], U8, name="w_scales", align_bytes=64)
+        qk_codes = resident.tile([P, PASSES * QK], U32, name="qk_codes", align_bytes=64)
+        qk_scales = resident.tile([P, PASSES * QK], U8, name="qk_scales", align_bytes=64)
+        qk_stage = resident.tile([P, N_BLOCKS, QK], F32, name="qk_stage")
+        identity = resident.tile([P, P], F32, name="identity")
+        gain_rows = resident.tile([P, 2 * P], BF16, name="gain_rows")
+        gain = resident.tile([P, PASSES * PACK], F32, name="gain")
+        minus_half = resident.tile([P, 1], F32, name="minus_half")
+        warm = resident.tile([P, 1], F32, name="warm")
+
+        def load_x(first, count):
+            blocks = slice(first, first + count)
+            nc.sync.dma_start(out=x_raw[:, blocks, :], in_=x_rows[:, blocks, :])
+
+        def load_w(first_row_block, count):
+            nc.sync.dma_start(
+                out=w_raw[:, first_row_block * K : (first_row_block + count) * K].rearrange(
+                    "p (i k) -> p i k", k=K
+                ),
+                in_=expand_w[first_row_block * P : (first_row_block + count) * P, :].rearrange(
+                    "(i p) k -> p i k", p=P
+                ),
+            )
+
+        def chunk_row_block(pair, half):
+            lin_first = QK // P + pair * CHUNK_ROW_BLOCKS
+            return lin_first if half == LIN else lin_first + E // P
+
+        affine = {}
+        normalised = {}
+        x_banks = {}
+        x_grouped = {}
+
+        def x_statistics(b):
+            stats = small.tile([P, 2, 6], F32, name="stats", tag="stats")
+            for h in range(2):
+                nc.vector.bn_stats(out=stats[:, h, :], in_=x_raw[:, b, h * 512 : (h + 1) * 512])
+            moments = small.tile([P, 3], F32, name="moments", tag="moments")
+            nc.vector.bn_aggr(out=moments[:, 0:2], in_=stats[:].rearrange("p h c -> p (h c)"))
+            nc.vector.tensor_scalar_add(out=moments[:, 2:3], in0=moments[:, 1:2], scalar1=EPS)
+            scale_bias = small.tile([P, 2], F32, name="scale_bias", tag="scale_bias")
+            nc.gpsimd.tensor_tensor(
+                out=scale_bias[:, 0:1], in0=moments[:, 2:3], in1=minus_half[:], op=ALU.pow
+            )
+            nc.gpsimd.tensor_scalar(
+                out=scale_bias[:, 1:2],
+                in0=moments[:, 0:1],
+                scalar1=scale_bias[:, 0:1],
+                scalar2=-1.0,
+                op0=ALU.mult,
+                op1=ALU.mult,
+            )
+            affine[b] = scale_bias
+
+        def x_normalise(b):
+            y = staging.tile([P, K], F32, name="y", tag="y")
+            nc.scalar.activation(
+                out=y[:].rearrange("p (a e q) -> p a e q", e=2, q=P),
+                in_=x_raw[:, b, :].rearrange("p (a q e) -> p a e q", e=2, q=P),
+                func=ACT.Identity,
+                bias=affine[b][:, 1:2],
+                scale=affine[b][:, 0:1],
+            )
+            normalised[b] = y
+
+        def x_transpose(b):
+            y = normalised[b]
+            x_banks[b] = []
+            for g in range(PASSES):
+                bank = work_banks.tile([P, PACK * P], F32, name="x_bank", tag="work")
+                for t in range(PACK):
+                    column = (g * PACK + t) * P
+                    nc.tensor.transpose(bank[:, t * P : (t + 1) * P], y[:, column : column + P], identity[:])
+                x_banks[b].append(bank)
+
+        def x_apply_gain(b):
+            grouped = staging.tile([P, PASSES * P * PACK], BF16, name="x_group", tag="x_group", align_bytes=64)
+            for g in range(PASSES):
+                nc.vector.tensor_tensor(
+                    out=grouped[:, g * P * PACK : (g + 1) * P * PACK].rearrange("p (r t) -> p r t", t=PACK),
+                    in0=x_banks[b][g][:].rearrange("p (t r) -> p r t", t=PACK),
+                    in1=gain[:, g * PACK : (g + 1) * PACK].unsqueeze(1).to_broadcast([P, P, PACK]),
+                    op=ALU.mult,
+                )
+            x_grouped[b] = grouped
+
+        def x_quantise(b):
+            columns = slice(b * PASSES * P, (b + 1) * PASSES * P)
+            nc.vector.quantize_mx(
+                out=x_codes[:, columns].bitcast(FP8X4), scales=x_scales[:, columns], in_=x_grouped[b][:]
+            )
+
+        def w_transpose(first_row_block, count):
+            grouped = staging.tile([P, PASSES * count * P * PACK], BF16, name="w_group", tag="w_group", align_bytes=64)
+            grouped_words = grouped[:].bitcast(F32).rearrange("p (g n u) -> p g n u", g=PASSES, u=2)
+            for i in range(count):
+                bank = work_banks.tile([P, PACK * P], F32, name="w_bank", tag="work")
+                for a in range(PACK):
+                    column = (first_row_block + i) * WORDS + a * P
+                    nc.tensor.transpose(bank[:, a * P : (a + 1) * P], w_words[:, column : column + P], identity[:])
+                source = bank[:].rearrange("p (g u r) -> p g r u", g=PASSES, u=2)
+                target = grouped_words[:, :, i * P : (i + 1) * P, :]
+                if i >= count - W_BANKS_ON_VECTOR:
+                    nc.vector.tensor_copy(out=target, in_=source)
+                else:
+                    nc.scalar.copy(out=target, in_=source)
+            return grouped
+
+        def w_quantise(grouped, codes, scales):
+            nc.vector.quantize_mx(out=codes.bitcast(FP8X4), scales=scales, in_=grouped[:])
+
+        def chunk_first_column(pair, half):
+            return (2 * pair + half) * PASSES * CHUNK
+
+        def chunk_transpose(pair, half):
+            return w_transpose(chunk_row_block(pair, half), CHUNK_ROW_BLOCKS)
+
+        def chunk_quantise(grouped, pair, half):
+            first = chunk_first_column(pair, half)
+            columns = slice(first, first + PASSES * CHUNK)
+            w_quantise(grouped, w_codes[:, columns], w_scales[:, columns])
+
+        def multiply(acc, b, codes, scales, first, width):
+            for g in range(PASSES):
+                rows = slice((b * PASSES + g) * P, (b * PASSES + g + 1) * P)
+                columns = slice(first + g * width, first + (g + 1) * width)
+                nc.tensor.matmul_mx(
+                    out=acc,
+                    lhsT=x_codes[:, rows].bitcast(FP8X4),
+                    lhsT_scale=x_scales[:, rows],
+                    rhs=codes[:, columns].bitcast(FP8X4),
+                    rhs_scale=scales[:, columns],
+                    start=(g == 0),
+                    stop=(g == PASSES - 1),
+                )
+
+        def project_qk(b):
+            acc = work_banks.tile([P, QK], F32, name="qk_acc", tag="work")
+            multiply(acc[:], b, qk_codes, qk_scales, 0, QK)
+            nc.scalar.copy(out=qk_stage[:, b, :], in_=acc[:])
+
+        def multiply_pair(b, pair):
+            pre = pre_banks.tile([P, CHUNK], F32, name="pre", tag="pre")
+            multiply(pre[:], b, w_codes, w_scales, chunk_first_column(pair, PRE), CHUNK)
+            lin = lin_banks.tile([P, CHUNK], F32, name="lin", tag="lin")
+            multiply(lin[:], b, w_codes, w_scales, chunk_first_column(pair, LIN), CHUNK)
+            gate = gated.tile([P, CHUNK], F32, name="gate", tag="gate")
+            nc.scalar.activation(out=gate[:], in_=pre[:], func=ACT.Gelu)
+            return b, pair, lin, gate
+
+        def gate_and_store(product):
+            b, pair, lin, gate = product
+            geglu = results.tile([P, CHUNK], F32, name="geglu", tag="geglu")
+            nc.vector.tensor_tensor(out=geglu[:], in0=lin[:], in1=gate[:], op=ALU.mult)
+            nc.sync.dma_start(out=geglu_rows[:, b, pair * CHUNK : (pair + 1) * CHUNK], in_=geglu[:])
+
+        nc.vector.memset(minus_half[:], -0.5)
+        nc.vector.memset(gain_rows[:].bitcast(F32), 0.0)
+        nc.scalar.dma_start(out=gain_rows[0:4, :], in_=norm_w.rearrange("(a c) -> a c", a=4))
+        nc.scalar.activation(out=warm[:], in_=minus_half[:], func=ACT.Gelu)
+        masks.make_identity(nc, identity[:])
+        gain_bank = work_banks.tile([P, P], F32, name="gain_bank", tag="work")
+        nc.tensor.transpose(gain_bank[:], gain_rows[:].bitcast(F32), identity[:])
+        nc.vector.tensor_copy(out=gain[:], in_=gain_bank[:, 0 : PASSES * 2].bitcast(BF16))
+
+        load_x(0, 1)
+        load_w(0, QK // P)
+        load_x(1, 1)
+        for pair in range(N_PAIRS):
+            if pair == N_PAIRS - 2:
+                load_x(FIRST_BLOCKS, 2)
+            load_w(chunk_row_block(pair, PRE), CHUNK_ROW_BLOCKS)
+            load_w(chunk_row_block(pair, LIN), CHUNK_ROW_BLOCKS)
+        load_x(FIRST_BLOCKS + 2, N_BLOCKS - FIRST_BLOCKS - 2)
+
+        x_statistics(0)
+        qk_grouped = w_transpose(0, QK // P)
+        x_normalise(0)
+        x_statistics(1)
+        x_transpose(0)
+        x_apply_gain(0)
+        x_normalise(1)
+        w_quantise(qk_grouped, qk_codes[:], qk_scales[:])
+        x_quantise(0)
+        grouped = chunk_transpose(0, PRE)
+        x_transpose(1)
+        x_apply_gain(1)
+        project_qk(0)
+        chunk_quantise(grouped, 0, PRE)
+        x_quantise(1)
+        grouped = chunk_transpose(0, LIN)
+        project_qk(1)
+        chunk_quantise(grouped, 0, LIN)
+
+        n_steps = N_PAIRS * FIRST_BLOCKS
+        chunk_waiting = None
+        product_waiting = None
+        for pair in range(N_PAIRS):
+            for b in range(FIRST_BLOCKS):
+                steps_left = n_steps - 1 - (pair * FIRST_BLOCKS + b)
+                if chunk_waiting is not None:
+                    chunk_quantise(*chunk_waiting)
+                    chunk_waiting = None
+                if product_waiting is not None:
+                    gate_and_store(product_waiting)
+                if steps_left == 3:
+                    x_statistics(FIRST_BLOCKS)
+                if steps_left == 2:
+                    x_normalise(FIRST_BLOCKS)
+                if steps_left == 1:
+                    x_transpose(FIRST_BLOCKS)
+                    x_apply_gain(FIRST_BLOCKS)
+                    x_statistics(FIRST_BLOCKS + 1)
+                if steps_left == 0:
+                    x_quantise(FIRST_BLOCKS)
+                    x_normalise(FIRST_BLOCKS + 1)
+                if pair + 1 < N_PAIRS:
+                    chunk_waiting = (chunk_transpose(pair + 1, b), pair + 1, b)
+                product_waiting = multiply_pair(b, pair)
+
+        for b in range(FIRST_BLOCKS, N_BLOCKS):
+            if b + 2 < N_BLOCKS:
+                x_statistics(b + 2)
+            project_qk(b)
+            if b == N_BLOCKS - 1:
+                nc.sync.dma_start(out=q_rows, in_=qk_stage[:, :, 0 : QK // 2])
+                nc.sync.dma_start(out=k_rows, in_=qk_stage[:, :, QK // 2 : QK])
+            for pair in range(N_PAIRS):
+                product = multiply_pair(b, pair)
+                gate_and_store(product_waiting)
+                product_waiting = product
+                if pair == 0 and b + 1 < N_BLOCKS:
+                    x_transpose(b + 1)
+                    x_apply_gain(b + 1)
+                if pair == 1 and b + 1 < N_BLOCKS:
+                    x_quantise(b + 1)
+                if pair == 2 and b + 2 < N_BLOCKS:
+                    x_normalise(b + 2)
+        gate_and_store(product_waiting)

@@ -21,13 +21,18 @@ N_BLOCKS = ROWS // P
 QK = 256
 E = 2048
 CHUNK = 512
-CHUNK_ROW_BLOCKS = CHUNK // P
 N_PAIRS = E // CHUNK
 PRE, LIN = 0, 1
-N_ROW_BLOCKS = (QK + 2 * E) // P
+QK_CHUNK = 2 * N_PAIRS
+HALF_BLOCKS = 2
+N_HALVES = 2 * QK_CHUNK + 1
 EPS = 1e-5
-FIRST_BLOCKS = 2
-W_BANKS_ON_VECTOR = 1
+FIRST_BLOCKS = 4
+STEPS = 4
+W_AHEAD = 4
+NORMALISE_AHEAD = 8
+TRANSPOSE_AHEAD = 3
+QUANTISE_AHEAD = 2
 
 FLOPS = 2 * ROWS * K * (QK + 2 * E)
 
@@ -37,7 +42,8 @@ def tile_latentattentionblock_pa_kernel(tc, x, norm_w, expand_w, out_0, out_1, o
     with ExitStack() as ctx:
         ctx.enter_context(tc.manual_schedule())
         resident = ctx.enter_context(tc.tile_pool(name="resident", bufs=1))
-        small = ctx.enter_context(tc.tile_pool(name="small", bufs=3))
+        small = ctx.enter_context(tc.tile_pool(name="small", bufs=4))
+        parted = ctx.enter_context(tc.tile_pool(name="parted", bufs=FIRST_BLOCKS))
         staging = ctx.enter_context(tc.tile_pool(name="staging", bufs=2))
         gated = ctx.enter_context(tc.tile_pool(name="gated", bufs=3))
         results = ctx.enter_context(tc.tile_pool(name="results", bufs=12))
@@ -51,14 +57,12 @@ def tile_latentattentionblock_pa_kernel(tc, x, norm_w, expand_w, out_0, out_1, o
         geglu_rows = out_2.rearrange("o (p i) d -> p (o i) d", i=N_BLOCKS)
 
         x_raw = resident.tile([P, N_BLOCKS, K], BF16, name="x_raw")
-        w_raw = resident.tile([P, N_ROW_BLOCKS * K], BF16, name="w_raw")
+        w_raw = resident.tile([P, (QK + 2 * E) // P * K], BF16, name="w_raw")
         w_words = w_raw[:].bitcast(F32)
         x_codes = resident.tile([P, N_BLOCKS * PASSES * P], U32, name="x_codes", align_bytes=64)
         x_scales = resident.tile([P, N_BLOCKS * PASSES * P], U8, name="x_scales", align_bytes=64)
-        w_codes = resident.tile([P, 2 * N_PAIRS * PASSES * CHUNK], U32, name="w_codes", align_bytes=64)
-        w_scales = resident.tile([P, 2 * N_PAIRS * PASSES * CHUNK], U8, name="w_scales", align_bytes=64)
-        qk_codes = resident.tile([P, PASSES * QK], U32, name="qk_codes", align_bytes=64)
-        qk_scales = resident.tile([P, PASSES * QK], U8, name="qk_scales", align_bytes=64)
+        w_codes = resident.tile([P, PASSES * (2 * E + QK)], U32, name="w_codes", align_bytes=64)
+        w_scales = resident.tile([P, PASSES * (2 * E + QK)], U8, name="w_scales", align_bytes=64)
         qk_stage = resident.tile([P, N_BLOCKS, QK], F32, name="qk_stage")
         identity = resident.tile([P, P], F32, name="identity")
         gain_rows = resident.tile([P, 2 * P], BF16, name="gain_rows")
@@ -70,6 +74,15 @@ def tile_latentattentionblock_pa_kernel(tc, x, norm_w, expand_w, out_0, out_1, o
             blocks = slice(first, first + count)
             nc.sync.dma_start(out=x_raw[:, blocks, :], in_=x_rows[:, blocks, :])
 
+        def chunk_width(chunk):
+            return QK if chunk == QK_CHUNK else CHUNK
+
+        def chunk_row_block(chunk):
+            if chunk == QK_CHUNK:
+                return 0
+            lin_first = (QK + chunk // 2 * CHUNK) // P
+            return lin_first if chunk % 2 == LIN else lin_first + E // P
+
         def load_w(first_row_block, count):
             nc.sync.dma_start(
                 out=w_raw[:, first_row_block * K : (first_row_block + count) * K].rearrange(
@@ -80,16 +93,15 @@ def tile_latentattentionblock_pa_kernel(tc, x, norm_w, expand_w, out_0, out_1, o
                 ),
             )
 
-        def chunk_row_block(pair, half):
-            lin_first = QK // P + pair * CHUNK_ROW_BLOCKS
-            return lin_first if half == LIN else lin_first + E // P
+        def load_chunk(chunk, pieces):
+            blocks = chunk_width(chunk) // P // pieces
+            for piece in range(pieces):
+                load_w(chunk_row_block(chunk) + piece * blocks, blocks)
 
-        affine = {}
         normalised = {}
-        x_banks = {}
         x_grouped = {}
 
-        def x_statistics(b):
+        def x_normalise(b):
             stats = small.tile([P, 2, 6], F32, name="stats", tag="stats")
             for h in range(2):
                 nc.vector.bn_stats(out=stats[:, h, :], in_=x_raw[:, b, h * 512 : (h + 1) * 512])
@@ -108,35 +120,28 @@ def tile_latentattentionblock_pa_kernel(tc, x, norm_w, expand_w, out_0, out_1, o
                 op0=ALU.mult,
                 op1=ALU.mult,
             )
-            affine[b] = scale_bias
-
-        def x_normalise(b):
-            y = staging.tile([P, K], F32, name="y", tag="y")
-            nc.scalar.activation(
+            y = parted.tile([P, K], F32, name="y", tag="y")
+            nc.gpsimd.tensor_scalar(
                 out=y[:].rearrange("p (a e q) -> p a e q", e=2, q=P),
-                in_=x_raw[:, b, :].rearrange("p (a q e) -> p a e q", e=2, q=P),
-                func=ACT.Identity,
-                bias=affine[b][:, 1:2],
-                scale=affine[b][:, 0:1],
+                in0=x_raw[:, b, :].rearrange("p (a q e) -> p a e q", e=2, q=P),
+                scalar1=scale_bias[:, 0:1],
+                scalar2=scale_bias[:, 1:2],
+                op0=ALU.mult,
+                op1=ALU.add,
             )
             normalised[b] = y
 
         def x_transpose(b):
             y = normalised[b]
-            x_banks[b] = []
+            grouped = staging.tile([P, PASSES * P * PACK], BF16, name="x_group", tag="x_group", align_bytes=64)
             for g in range(PASSES):
                 bank = work_banks.tile([P, PACK * P], F32, name="x_bank", tag="work")
                 for t in range(PACK):
                     column = (g * PACK + t) * P
                     nc.tensor.transpose(bank[:, t * P : (t + 1) * P], y[:, column : column + P], identity[:])
-                x_banks[b].append(bank)
-
-        def x_apply_gain(b):
-            grouped = staging.tile([P, PASSES * P * PACK], BF16, name="x_group", tag="x_group", align_bytes=64)
-            for g in range(PASSES):
                 nc.vector.tensor_tensor(
                     out=grouped[:, g * P * PACK : (g + 1) * P * PACK].rearrange("p (r t) -> p r t", t=PACK),
-                    in0=x_banks[b][g][:].rearrange("p (t r) -> p r t", t=PACK),
+                    in0=bank[:].rearrange("p (t r) -> p r t", t=PACK),
                     in1=gain[:, g * PACK : (g + 1) * PACK].unsqueeze(1).to_broadcast([P, P, PACK]),
                     op=ALU.mult,
                 )
@@ -148,60 +153,65 @@ def tile_latentattentionblock_pa_kernel(tc, x, norm_w, expand_w, out_0, out_1, o
                 out=x_codes[:, columns].bitcast(FP8X4), scales=x_scales[:, columns], in_=x_grouped[b][:]
             )
 
-        def w_transpose(first_row_block, count):
-            grouped = staging.tile([P, PASSES * count * P * PACK], BF16, name="w_group", tag="w_group", align_bytes=64)
-            grouped_words = grouped[:].bitcast(F32).rearrange("p (g n u) -> p g n u", g=PASSES, u=2)
-            for i in range(count):
+        w_grouped = {}
+
+        def w_transpose(half):
+            chunk = half // 2
+            width = chunk_width(chunk)
+            if half % 2 == 0:
+                w_grouped[chunk] = staging.tile(
+                    [P, PASSES * width * PACK], BF16, name="w_group", tag="w_group", align_bytes=64
+                )
+            grouped_words = w_grouped[chunk][:].bitcast(F32).rearrange("p (g n u) -> p g n u", g=PASSES, u=2)
+            for i in range(HALF_BLOCKS):
+                block = half % 2 * HALF_BLOCKS + i
                 bank = work_banks.tile([P, PACK * P], F32, name="w_bank", tag="work")
                 for a in range(PACK):
-                    column = (first_row_block + i) * WORDS + a * P
+                    column = (chunk_row_block(chunk) + block) * WORDS + a * P
                     nc.tensor.transpose(bank[:, a * P : (a + 1) * P], w_words[:, column : column + P], identity[:])
                 source = bank[:].rearrange("p (g u r) -> p g r u", g=PASSES, u=2)
-                target = grouped_words[:, :, i * P : (i + 1) * P, :]
-                if i >= count - W_BANKS_ON_VECTOR:
-                    nc.vector.tensor_copy(out=target, in_=source)
-                else:
-                    nc.scalar.copy(out=target, in_=source)
-            return grouped
+                target = grouped_words[:, :, block * P : (block + 1) * P, :]
+                nc.scalar.copy(out=target, in_=source)
 
-        def w_quantise(grouped, codes, scales):
-            nc.vector.quantize_mx(out=codes.bitcast(FP8X4), scales=scales, in_=grouped[:])
+        def chunk_columns(chunk):
+            first = chunk * PASSES * CHUNK
+            return slice(first, first + PASSES * chunk_width(chunk))
 
-        def chunk_first_column(pair, half):
-            return (2 * pair + half) * PASSES * CHUNK
+        def w_quantise(chunk):
+            columns = chunk_columns(chunk)
+            nc.vector.quantize_mx(
+                out=w_codes[:, columns].bitcast(FP8X4), scales=w_scales[:, columns], in_=w_grouped[chunk][:]
+            )
 
-        def chunk_transpose(pair, half):
-            return w_transpose(chunk_row_block(pair, half), CHUNK_ROW_BLOCKS)
+        def completes_chunk(half):
+            return 0 <= half < N_HALVES and (half % 2 == 1 or half // 2 == QK_CHUNK)
 
-        def chunk_quantise(grouped, pair, half):
-            first = chunk_first_column(pair, half)
-            columns = slice(first, first + PASSES * CHUNK)
-            w_quantise(grouped, w_codes[:, columns], w_scales[:, columns])
-
-        def multiply(acc, b, codes, scales, first, width):
+        def multiply(acc, b, chunk):
+            width = chunk_width(chunk)
             for g in range(PASSES):
                 rows = slice((b * PASSES + g) * P, (b * PASSES + g + 1) * P)
-                columns = slice(first + g * width, first + (g + 1) * width)
+                first = chunk * PASSES * CHUNK + g * width
+                columns = slice(first, first + width)
                 nc.tensor.matmul_mx(
                     out=acc,
                     lhsT=x_codes[:, rows].bitcast(FP8X4),
                     lhsT_scale=x_scales[:, rows],
-                    rhs=codes[:, columns].bitcast(FP8X4),
-                    rhs_scale=scales[:, columns],
+                    rhs=w_codes[:, columns].bitcast(FP8X4),
+                    rhs_scale=w_scales[:, columns],
                     start=(g == 0),
                     stop=(g == PASSES - 1),
                 )
 
         def project_qk(b):
             acc = work_banks.tile([P, QK], F32, name="qk_acc", tag="work")
-            multiply(acc[:], b, qk_codes, qk_scales, 0, QK)
+            multiply(acc[:], b, QK_CHUNK)
             nc.scalar.copy(out=qk_stage[:, b, :], in_=acc[:])
 
         def multiply_pair(b, pair):
             pre = pre_banks.tile([P, CHUNK], F32, name="pre", tag="pre")
-            multiply(pre[:], b, w_codes, w_scales, chunk_first_column(pair, PRE), CHUNK)
+            multiply(pre[:], b, 2 * pair + PRE)
             lin = lin_banks.tile([P, CHUNK], F32, name="lin", tag="lin")
-            multiply(lin[:], b, w_codes, w_scales, chunk_first_column(pair, LIN), CHUNK)
+            multiply(lin[:], b, 2 * pair + LIN)
             gate = gated.tile([P, CHUNK], F32, name="gate", tag="gate")
             nc.scalar.activation(out=gate[:], in_=pre[:], func=ACT.Gelu)
             return b, pair, lin, gate
@@ -212,86 +222,59 @@ def tile_latentattentionblock_pa_kernel(tc, x, norm_w, expand_w, out_0, out_1, o
             nc.vector.tensor_tensor(out=geglu[:], in0=lin[:], in1=gate[:], op=ALU.mult)
             nc.sync.dma_start(out=geglu_rows[:, b, pair * CHUNK : (pair + 1) * CHUNK], in_=geglu[:])
 
-        nc.vector.memset(minus_half[:], -0.5)
         nc.vector.memset(gain_rows[:].bitcast(F32), 0.0)
-        nc.scalar.dma_start(out=gain_rows[0:4, :], in_=norm_w.rearrange("(a c) -> a c", a=4))
+        nc.vector.memset(minus_half[:], -0.5)
+        nc.sync.dma_start(out=gain_rows[0:4, :], in_=norm_w.rearrange("(a c) -> a c", a=4))
         nc.scalar.activation(out=warm[:], in_=minus_half[:], func=ACT.Gelu)
         masks.make_identity(nc, identity[:])
-        gain_bank = work_banks.tile([P, P], F32, name="gain_bank", tag="work")
-        nc.tensor.transpose(gain_bank[:], gain_rows[:].bitcast(F32), identity[:])
-        nc.vector.tensor_copy(out=gain[:], in_=gain_bank[:, 0 : PASSES * 2].bitcast(BF16))
 
-        load_x(0, 1)
-        load_w(0, QK // P)
-        load_x(1, 1)
-        for pair in range(N_PAIRS):
-            if pair == N_PAIRS - 2:
-                load_x(FIRST_BLOCKS, 2)
-            load_w(chunk_row_block(pair, PRE), CHUNK_ROW_BLOCKS)
-            load_w(chunk_row_block(pair, LIN), CHUNK_ROW_BLOCKS)
-        load_x(FIRST_BLOCKS + 2, N_BLOCKS - FIRST_BLOCKS - 2)
+        load_x(0, 2)
+        load_x(2, 2)
+        load_chunk(0, 2)
+        load_chunk(1, 2)
+        for chunk in range(2, QK_CHUNK + 1):
+            load_chunk(chunk, 1)
+            if chunk == 3:
+                load_x(FIRST_BLOCKS, N_BLOCKS - FIRST_BLOCKS)
 
-        x_statistics(0)
-        qk_grouped = w_transpose(0, QK // P)
-        x_normalise(0)
-        x_statistics(1)
-        x_transpose(0)
-        x_apply_gain(0)
-        x_normalise(1)
-        w_quantise(qk_grouped, qk_codes[:], qk_scales[:])
-        x_quantise(0)
-        grouped = chunk_transpose(0, PRE)
-        x_transpose(1)
-        x_apply_gain(1)
-        project_qk(0)
-        chunk_quantise(grouped, 0, PRE)
-        x_quantise(1)
-        grouped = chunk_transpose(0, LIN)
-        project_qk(1)
-        chunk_quantise(grouped, 0, LIN)
+        def spread_gain():
+            gain_bank = work_banks.tile([P, P], F32, name="gain_bank", tag="work")
+            nc.tensor.transpose(gain_bank[:], gain_rows[:].bitcast(F32), identity[:])
+            nc.vector.tensor_copy(out=gain[:], in_=gain_bank[:, 0 : PASSES * 2].bitcast(BF16))
 
-        n_steps = N_PAIRS * FIRST_BLOCKS
-        chunk_waiting = None
+        def block_starting_at(n):
+            if 0 <= n < FIRST_BLOCKS:
+                return n
+            if n % STEPS == 0 and FIRST_BLOCKS <= n // STEPS < N_BLOCKS:
+                return n // STEPS
+            return None
+
         product_waiting = None
-        for pair in range(N_PAIRS):
-            for b in range(FIRST_BLOCKS):
-                steps_left = n_steps - 1 - (pair * FIRST_BLOCKS + b)
-                if chunk_waiting is not None:
-                    chunk_quantise(*chunk_waiting)
-                    chunk_waiting = None
-                if product_waiting is not None:
-                    gate_and_store(product_waiting)
-                if steps_left == 3:
-                    x_statistics(FIRST_BLOCKS)
-                if steps_left == 2:
-                    x_normalise(FIRST_BLOCKS)
-                if steps_left == 1:
-                    x_transpose(FIRST_BLOCKS)
-                    x_apply_gain(FIRST_BLOCKS)
-                    x_statistics(FIRST_BLOCKS + 1)
-                if steps_left == 0:
-                    x_quantise(FIRST_BLOCKS)
-                    x_normalise(FIRST_BLOCKS + 1)
-                if pair + 1 < N_PAIRS:
-                    chunk_waiting = (chunk_transpose(pair + 1, b), pair + 1, b)
-                product_waiting = multiply_pair(b, pair)
-
-        for b in range(FIRST_BLOCKS, N_BLOCKS):
-            if b + 2 < N_BLOCKS:
-                x_statistics(b + 2)
-            project_qk(b)
-            if b == N_BLOCKS - 1:
+        for n in range(-max(NORMALISE_AHEAD, W_AHEAD), N_BLOCKS * STEPS):
+            rnd, step = n // STEPS, n % STEPS
+            half = n + W_AHEAD
+            if completes_chunk(half - 1):
+                w_quantise((half - 1) // 2)
+            if product_waiting is not None:
+                gate_and_store(product_waiting)
+                product_waiting = None
+            if block_starting_at(n + NORMALISE_AHEAD) is not None:
+                x_normalise(block_starting_at(n + NORMALISE_AHEAD))
+            if step == 0 and rnd >= FIRST_BLOCKS:
+                project_qk(rnd - FIRST_BLOCKS)
+                project_qk(rnd)
+            if step == 0 and rnd == N_BLOCKS - 1:
                 nc.sync.dma_start(out=q_rows, in_=qk_stage[:, :, 0 : QK // 2])
                 nc.sync.dma_start(out=k_rows, in_=qk_stage[:, :, QK // 2 : QK])
-            for pair in range(N_PAIRS):
-                product = multiply_pair(b, pair)
-                gate_and_store(product_waiting)
-                product_waiting = product
-                if pair == 0 and b + 1 < N_BLOCKS:
-                    x_transpose(b + 1)
-                    x_apply_gain(b + 1)
-                if pair == 1 and b + 1 < N_BLOCKS:
-                    x_quantise(b + 1)
-                if pair == 2 and b + 2 < N_BLOCKS:
-                    x_normalise(b + 2)
+            if 0 <= half < N_HALVES:
+                w_transpose(half)
+            if n + TRANSPOSE_AHEAD == 0:
+                spread_gain()
+            if block_starting_at(n + TRANSPOSE_AHEAD) is not None:
+                x_transpose(block_starting_at(n + TRANSPOSE_AHEAD))
+            if block_starting_at(n + QUANTISE_AHEAD) is not None:
+                x_quantise(block_starting_at(n + QUANTISE_AHEAD))
+            if n >= 0:
+                b, pair = (step, rnd) if rnd < FIRST_BLOCKS else (rnd, step)
+                product_waiting = multiply_pair(b, pair)
         gate_and_store(product_waiting)

@@ -18,19 +18,24 @@ PASSES = K // (P * PACK)
 WORDS = K // 2
 ROWS = 1024
 N_BLOCKS = ROWS // P
-QK = 256
+HEAD = 128
+QK = 2 * HEAD
 E = 2048
 CHUNK = 512
 N_PAIRS = E // CHUNK
 PRE, LIN = 0, 1
 QK_CHUNK = 2 * N_PAIRS
-HALF_BLOCKS = 2
-N_HALVES = 2 * QK_CHUNK + 1
+RUN_ROW_BLOCKS = 2
+N_RUNS = 2 * QK_CHUNK + 1
+BN_STATS_MAX = 512
 EPS = 1e-5
+N_BANKS = 8
+
 FIRST_BLOCKS = 4
 STEPS = 4
-W_AHEAD = 4
-NORMALISE_AHEAD = 8
+N_PRODUCTS = N_BLOCKS * N_PAIRS
+RUNS_AHEAD = 4
+STATISTICS_AHEAD = 8
 TRANSPOSE_AHEAD = 3
 QUANTISE_AHEAD = 2
 
@@ -42,14 +47,11 @@ def tile_latentattentionblock_pa_kernel(tc, x, norm_w, expand_w, out_0, out_1, o
     with ExitStack() as ctx:
         ctx.enter_context(tc.manual_schedule())
         resident = ctx.enter_context(tc.tile_pool(name="resident", bufs=1))
-        small = ctx.enter_context(tc.tile_pool(name="small", bufs=4))
-        parted = ctx.enter_context(tc.tile_pool(name="parted", bufs=FIRST_BLOCKS))
-        staging = ctx.enter_context(tc.tile_pool(name="staging", bufs=2))
-        gated = ctx.enter_context(tc.tile_pool(name="gated", bufs=3))
+        per_block = ctx.enter_context(tc.tile_pool(name="per_block", bufs=FIRST_BLOCKS))
+        grouped_tiles = ctx.enter_context(tc.tile_pool(name="grouped_tiles", bufs=2))
+        gates = ctx.enter_context(tc.tile_pool(name="gates", bufs=N_BANKS // 2 + 1))
         results = ctx.enter_context(tc.tile_pool(name="results", bufs=12))
-        work_banks = ctx.enter_context(tc.psum_pool(name="work_banks", bufs=3))
-        pre_banks = ctx.enter_context(tc.psum_pool(name="pre_banks", bufs=2))
-        lin_banks = ctx.enter_context(tc.psum_pool(name="lin_banks", bufs=3))
+        banks = ctx.enter_context(tc.psum_pool(name="banks", bufs=N_BANKS))
 
         x_rows = x.rearrange("o (p i) w -> p (o i) w", i=N_BLOCKS)
         q_rows = out_0.rearrange("o (p i) d -> p (o i) d", i=N_BLOCKS)
@@ -63,7 +65,7 @@ def tile_latentattentionblock_pa_kernel(tc, x, norm_w, expand_w, out_0, out_1, o
         x_scales = resident.tile([P, N_BLOCKS * PASSES * P], U8, name="x_scales", align_bytes=64)
         w_codes = resident.tile([P, PASSES * (2 * E + QK)], U32, name="w_codes", align_bytes=64)
         w_scales = resident.tile([P, PASSES * (2 * E + QK)], U8, name="w_scales", align_bytes=64)
-        qk_stage = resident.tile([P, N_BLOCKS, QK], F32, name="qk_stage")
+        qk_stage = resident.tile([P, 2, N_BLOCKS, HEAD], F32, name="qk_stage")
         identity = resident.tile([P, P], F32, name="identity")
         gain_rows = resident.tile([P, 2 * P], BF16, name="gain_rows")
         gain = resident.tile([P, PASSES * PACK], F32, name="gain")
@@ -83,35 +85,27 @@ def tile_latentattentionblock_pa_kernel(tc, x, norm_w, expand_w, out_0, out_1, o
             lin_first = (QK + chunk // 2 * CHUNK) // P
             return lin_first if chunk % 2 == LIN else lin_first + E // P
 
-        def load_w(first_row_block, count):
-            nc.sync.dma_start(
-                out=w_raw[:, first_row_block * K : (first_row_block + count) * K].rearrange(
-                    "p (i k) -> p i k", k=K
-                ),
-                in_=expand_w[first_row_block * P : (first_row_block + count) * P, :].rearrange(
-                    "(i p) k -> p i k", p=P
-                ),
-            )
-
         def load_chunk(chunk, pieces):
-            blocks = chunk_width(chunk) // P // pieces
+            count = chunk_width(chunk) // P // pieces
             for piece in range(pieces):
-                load_w(chunk_row_block(chunk) + piece * blocks, blocks)
+                first = chunk_row_block(chunk) + piece * count
+                nc.sync.dma_start(
+                    out=w_raw[:, first * K : (first + count) * K].rearrange("p (i k) -> p i k", k=K),
+                    in_=expand_w[first * P : (first + count) * P, :].rearrange("(i p) k -> p i k", p=P),
+                )
 
         normalised = {}
         x_grouped = {}
 
         def x_normalise(b):
-            stats = small.tile([P, 2, 6], F32, name="stats", tag="stats")
-            for h in range(2):
-                nc.vector.bn_stats(out=stats[:, h, :], in_=x_raw[:, b, h * 512 : (h + 1) * 512])
-            moments = small.tile([P, 3], F32, name="moments", tag="moments")
+            stats = per_block.tile([P, K // BN_STATS_MAX, 6], F32, name="stats", tag="stats")
+            for h in range(K // BN_STATS_MAX):
+                nc.vector.bn_stats(out=stats[:, h, :], in_=x_raw[:, b, h * BN_STATS_MAX : (h + 1) * BN_STATS_MAX])
+            moments = per_block.tile([P, 3], F32, name="moments", tag="moments")
             nc.vector.bn_aggr(out=moments[:, 0:2], in_=stats[:].rearrange("p h c -> p (h c)"))
             nc.vector.tensor_scalar_add(out=moments[:, 2:3], in0=moments[:, 1:2], scalar1=EPS)
-            scale_bias = small.tile([P, 2], F32, name="scale_bias", tag="scale_bias")
-            nc.gpsimd.tensor_tensor(
-                out=scale_bias[:, 0:1], in0=moments[:, 2:3], in1=minus_half[:], op=ALU.pow
-            )
+            scale_bias = per_block.tile([P, 2], F32, name="scale_bias", tag="scale_bias")
+            nc.gpsimd.tensor_tensor(out=scale_bias[:, 0:1], in0=moments[:, 2:3], in1=minus_half[:], op=ALU.pow)
             nc.gpsimd.tensor_scalar(
                 out=scale_bias[:, 1:2],
                 in0=moments[:, 0:1],
@@ -120,7 +114,7 @@ def tile_latentattentionblock_pa_kernel(tc, x, norm_w, expand_w, out_0, out_1, o
                 op0=ALU.mult,
                 op1=ALU.mult,
             )
-            y = parted.tile([P, K], F32, name="y", tag="y")
+            y = per_block.tile([P, K], F32, name="y", tag="y")
             nc.gpsimd.tensor_scalar(
                 out=y[:].rearrange("p (a e q) -> p a e q", e=2, q=P),
                 in0=x_raw[:, b, :].rearrange("p (a q e) -> p a e q", e=2, q=P),
@@ -131,11 +125,16 @@ def tile_latentattentionblock_pa_kernel(tc, x, norm_w, expand_w, out_0, out_1, o
             )
             normalised[b] = y
 
+        def spread_gain():
+            gain_bank = banks.tile([P, P], F32, name="gain_bank", tag="bank")
+            nc.tensor.transpose(gain_bank[:], gain_rows[:].bitcast(F32), identity[:])
+            nc.vector.tensor_copy(out=gain[:], in_=gain_bank[:, 0 : PASSES * 2].bitcast(BF16))
+
         def x_transpose(b):
             y = normalised[b]
-            grouped = staging.tile([P, PASSES * P * PACK], BF16, name="x_group", tag="x_group", align_bytes=64)
+            grouped = grouped_tiles.tile([P, PASSES * P * PACK], BF16, name="x_grouped", tag="x", align_bytes=64)
             for g in range(PASSES):
-                bank = work_banks.tile([P, PACK * P], F32, name="x_bank", tag="work")
+                bank = banks.tile([P, PACK * P], F32, name="x_bank", tag="bank")
                 for t in range(PACK):
                     column = (g * PACK + t) * P
                     nc.tensor.transpose(bank[:, t * P : (t + 1) * P], y[:, column : column + P], identity[:])
@@ -155,36 +154,33 @@ def tile_latentattentionblock_pa_kernel(tc, x, norm_w, expand_w, out_0, out_1, o
 
         w_grouped = {}
 
-        def w_transpose(half):
-            chunk = half // 2
-            width = chunk_width(chunk)
-            if half % 2 == 0:
-                w_grouped[chunk] = staging.tile(
-                    [P, PASSES * width * PACK], BF16, name="w_group", tag="w_group", align_bytes=64
+        def w_transpose(run):
+            chunk = run // 2
+            if run % 2 == 0:
+                w_grouped[chunk] = grouped_tiles.tile(
+                    [P, PASSES * chunk_width(chunk) * PACK], BF16, name="w_grouped", tag="w", align_bytes=64
                 )
             grouped_words = w_grouped[chunk][:].bitcast(F32).rearrange("p (g n u) -> p g n u", g=PASSES, u=2)
-            for i in range(HALF_BLOCKS):
-                block = half % 2 * HALF_BLOCKS + i
-                bank = work_banks.tile([P, PACK * P], F32, name="w_bank", tag="work")
+            for i in range(RUN_ROW_BLOCKS):
+                block = run % 2 * RUN_ROW_BLOCKS + i
+                bank = banks.tile([P, PACK * P], F32, name="w_bank", tag="bank")
                 for a in range(PACK):
                     column = (chunk_row_block(chunk) + block) * WORDS + a * P
                     nc.tensor.transpose(bank[:, a * P : (a + 1) * P], w_words[:, column : column + P], identity[:])
-                source = bank[:].rearrange("p (g u r) -> p g r u", g=PASSES, u=2)
-                target = grouped_words[:, :, block * P : (block + 1) * P, :]
-                nc.scalar.copy(out=target, in_=source)
+                nc.scalar.copy(
+                    out=grouped_words[:, :, block * P : (block + 1) * P, :],
+                    in_=bank[:].rearrange("p (g u r) -> p g r u", g=PASSES, u=2),
+                )
 
-        def chunk_columns(chunk):
-            first = chunk * PASSES * CHUNK
-            return slice(first, first + PASSES * chunk_width(chunk))
+        def completes_chunk(run):
+            return 0 <= run < N_RUNS and (run % 2 == 1 or run // 2 == QK_CHUNK)
 
         def w_quantise(chunk):
-            columns = chunk_columns(chunk)
+            first = chunk * PASSES * CHUNK
+            columns = slice(first, first + PASSES * chunk_width(chunk))
             nc.vector.quantize_mx(
                 out=w_codes[:, columns].bitcast(FP8X4), scales=w_scales[:, columns], in_=w_grouped[chunk][:]
             )
-
-        def completes_chunk(half):
-            return 0 <= half < N_HALVES and (half % 2 == 1 or half // 2 == QK_CHUNK)
 
         def multiply(acc, b, chunk):
             width = chunk_width(chunk)
@@ -203,16 +199,16 @@ def tile_latentattentionblock_pa_kernel(tc, x, norm_w, expand_w, out_0, out_1, o
                 )
 
         def project_qk(b):
-            acc = work_banks.tile([P, QK], F32, name="qk_acc", tag="work")
+            acc = banks.tile([P, QK], F32, name="qk_acc", tag="bank")
             multiply(acc[:], b, QK_CHUNK)
-            nc.scalar.copy(out=qk_stage[:, b, :], in_=acc[:])
+            nc.scalar.copy(out=qk_stage[:, :, b, :], in_=acc[:].rearrange("p (h d) -> p h d", h=2))
 
         def multiply_pair(b, pair):
-            pre = pre_banks.tile([P, CHUNK], F32, name="pre", tag="pre")
+            pre = banks.tile([P, CHUNK], F32, name="pre", tag="bank")
             multiply(pre[:], b, 2 * pair + PRE)
-            lin = lin_banks.tile([P, CHUNK], F32, name="lin", tag="lin")
+            lin = banks.tile([P, CHUNK], F32, name="lin", tag="bank")
             multiply(lin[:], b, 2 * pair + LIN)
-            gate = gated.tile([P, CHUNK], F32, name="gate", tag="gate")
+            gate = gates.tile([P, CHUNK], F32, name="gate", tag="gate")
             nc.scalar.activation(out=gate[:], in_=pre[:], func=ACT.Gelu)
             return b, pair, lin, gate
 
@@ -224,23 +220,17 @@ def tile_latentattentionblock_pa_kernel(tc, x, norm_w, expand_w, out_0, out_1, o
 
         nc.vector.memset(gain_rows[:].bitcast(F32), 0.0)
         nc.vector.memset(minus_half[:], -0.5)
-        nc.sync.dma_start(out=gain_rows[0:4, :], in_=norm_w.rearrange("(a c) -> a c", a=4))
         nc.scalar.activation(out=warm[:], in_=minus_half[:], func=ACT.Gelu)
         masks.make_identity(nc, identity[:])
 
-        load_x(0, 2)
-        load_x(2, 2)
-        load_chunk(0, 2)
-        load_chunk(1, 2)
-        for chunk in range(2, QK_CHUNK + 1):
-            load_chunk(chunk, 1)
-            if chunk == 3:
+        load_x(0, 1)
+        nc.sync.dma_start(out=gain_rows[0:4, :], in_=norm_w.rearrange("(a c) -> a c", a=4))
+        for b in range(1, FIRST_BLOCKS):
+            load_x(b, 1)
+        for chunk in range(QK_CHUNK + 1):
+            load_chunk(chunk, 2 if chunk // 2 == 0 else 1)
+            if chunk == 2 * 1 + LIN:
                 load_x(FIRST_BLOCKS, N_BLOCKS - FIRST_BLOCKS)
-
-        def spread_gain():
-            gain_bank = work_banks.tile([P, P], F32, name="gain_bank", tag="work")
-            nc.tensor.transpose(gain_bank[:], gain_rows[:].bitcast(F32), identity[:])
-            nc.vector.tensor_copy(out=gain[:], in_=gain_bank[:, 0 : PASSES * 2].bitcast(BF16))
 
         def block_starting_at(n):
             if 0 <= n < FIRST_BLOCKS:
@@ -250,24 +240,23 @@ def tile_latentattentionblock_pa_kernel(tc, x, norm_w, expand_w, out_0, out_1, o
             return None
 
         product_waiting = None
-        for n in range(-max(NORMALISE_AHEAD, W_AHEAD), N_BLOCKS * STEPS):
+        for n in range(-STATISTICS_AHEAD, N_PRODUCTS):
             rnd, step = n // STEPS, n % STEPS
-            half = n + W_AHEAD
-            if completes_chunk(half - 1):
-                w_quantise((half - 1) // 2)
+            run = n + RUNS_AHEAD
+            if completes_chunk(run - 1):
+                w_quantise((run - 1) // 2)
             if product_waiting is not None:
                 gate_and_store(product_waiting)
-                product_waiting = None
-            if block_starting_at(n + NORMALISE_AHEAD) is not None:
-                x_normalise(block_starting_at(n + NORMALISE_AHEAD))
+            if block_starting_at(n + STATISTICS_AHEAD) is not None:
+                x_normalise(block_starting_at(n + STATISTICS_AHEAD))
             if step == 0 and rnd >= FIRST_BLOCKS:
                 project_qk(rnd - FIRST_BLOCKS)
                 project_qk(rnd)
-            if step == 0 and rnd == N_BLOCKS - 1:
-                nc.sync.dma_start(out=q_rows, in_=qk_stage[:, :, 0 : QK // 2])
-                nc.sync.dma_start(out=k_rows, in_=qk_stage[:, :, QK // 2 : QK])
-            if 0 <= half < N_HALVES:
-                w_transpose(half)
+            if n == N_PRODUCTS - STEPS:
+                nc.sync.dma_start(out=q_rows, in_=qk_stage[:, 0, :, :])
+                nc.sync.dma_start(out=k_rows, in_=qk_stage[:, 1, :, :])
+            if 0 <= run < N_RUNS:
+                w_transpose(run)
             if n + TRANSPOSE_AHEAD == 0:
                 spread_gain()
             if block_starting_at(n + TRANSPOSE_AHEAD) is not None:

@@ -34,10 +34,10 @@ N_BANKS = 8
 FIRST_BLOCKS = 4
 STEPS = 4
 N_PRODUCTS = N_BLOCKS * N_PAIRS
-RUNS_AHEAD = 4
-STATISTICS_AHEAD = 8
-TRANSPOSE_AHEAD = 3
-QUANTISE_AHEAD = 2
+RUNS_AHEAD = 5
+STATISTICS_AHEAD = 12
+TRANSPOSE_AHEAD = 5
+QUANTISE_AHEAD = 4
 
 FLOPS = 2 * ROWS * K * (QK + 2 * E)
 
@@ -172,15 +172,17 @@ def tile_latentattentionblock_pa_kernel(tc, x, norm_w, expand_w, out_0, out_1, o
                     in_=bank[:].rearrange("p (g u r) -> p g r u", g=PASSES, u=2),
                 )
 
-        def completes_chunk(run):
-            return 0 <= run < N_RUNS and (run % 2 == 1 or run // 2 == QK_CHUNK)
-
-        def w_quantise(chunk):
-            first = chunk * PASSES * CHUNK
-            columns = slice(first, first + PASSES * chunk_width(chunk))
-            nc.vector.quantize_mx(
-                out=w_codes[:, columns].bitcast(FP8X4), scales=w_scales[:, columns], in_=w_grouped[chunk][:]
-            )
+        def w_quantise(run):
+            chunk = run // 2
+            width = chunk_width(chunk)
+            for g in range(PASSES):
+                first = g * width + run % 2 * RUN_ROW_BLOCKS * P
+                columns = slice(chunk * PASSES * CHUNK + first, chunk * PASSES * CHUNK + first + RUN_ROW_BLOCKS * P)
+                nc.vector.quantize_mx(
+                    out=w_codes[:, columns].bitcast(FP8X4),
+                    scales=w_scales[:, columns],
+                    in_=w_grouped[chunk][:, first * PACK : (first + RUN_ROW_BLOCKS * P) * PACK],
+                )
 
         def multiply(acc, b, chunk):
             width = chunk_width(chunk)
@@ -243,8 +245,8 @@ def tile_latentattentionblock_pa_kernel(tc, x, norm_w, expand_w, out_0, out_1, o
         for n in range(-STATISTICS_AHEAD, N_PRODUCTS):
             rnd, step = n // STEPS, n % STEPS
             run = n + RUNS_AHEAD
-            if completes_chunk(run - 1):
-                w_quantise((run - 1) // 2)
+            if 0 <= run - 1 < N_RUNS:
+                w_quantise(run - 1)
             if product_waiting is not None:
                 gate_and_store(product_waiting)
             if block_starting_at(n + STATISTICS_AHEAD) is not None:

@@ -34,10 +34,10 @@ N_BANKS = 8
 FIRST_BLOCKS = 4
 STEPS = 4
 N_PRODUCTS = N_BLOCKS * N_PAIRS
-RUNS_AHEAD = 5
-STATISTICS_AHEAD = 12
-TRANSPOSE_AHEAD = 5
-QUANTISE_AHEAD = 4
+RUNS_AHEAD = 4
+STATISTICS_AHEAD = 8
+TRANSPOSE_AHEAD = 3
+QUANTISE_AHEAD = 2
 
 FLOPS = 2 * ROWS * K * (QK + 2 * E)
 
@@ -45,7 +45,6 @@ FLOPS = 2 * ROWS * K * (QK + 2 * E)
 def tile_latentattentionblock_pa_kernel(tc, x, norm_w, expand_w, out_0, out_1, out_2):
     nc = tc.nc
     with ExitStack() as ctx:
-        ctx.enter_context(tc.manual_schedule())
         resident = ctx.enter_context(tc.tile_pool(name="resident", bufs=1))
         per_block = ctx.enter_context(tc.tile_pool(name="per_block", bufs=FIRST_BLOCKS))
         grouped_tiles = ctx.enter_context(tc.tile_pool(name="grouped_tiles", bufs=2))
@@ -172,17 +171,15 @@ def tile_latentattentionblock_pa_kernel(tc, x, norm_w, expand_w, out_0, out_1, o
                     in_=bank[:].rearrange("p (g u r) -> p g r u", g=PASSES, u=2),
                 )
 
-        def w_quantise(run):
-            chunk = run // 2
-            width = chunk_width(chunk)
-            for g in range(PASSES):
-                first = g * width + run % 2 * RUN_ROW_BLOCKS * P
-                columns = slice(chunk * PASSES * CHUNK + first, chunk * PASSES * CHUNK + first + RUN_ROW_BLOCKS * P)
-                nc.vector.quantize_mx(
-                    out=w_codes[:, columns].bitcast(FP8X4),
-                    scales=w_scales[:, columns],
-                    in_=w_grouped[chunk][:, first * PACK : (first + RUN_ROW_BLOCKS * P) * PACK],
-                )
+        def completes_chunk(run):
+            return 0 <= run < N_RUNS and (run % 2 == 1 or run // 2 == QK_CHUNK)
+
+        def w_quantise(chunk):
+            first = chunk * PASSES * CHUNK
+            columns = slice(first, first + PASSES * chunk_width(chunk))
+            nc.vector.quantize_mx(
+                out=w_codes[:, columns].bitcast(FP8X4), scales=w_scales[:, columns], in_=w_grouped[chunk][:]
+            )
 
         def multiply(acc, b, chunk):
             width = chunk_width(chunk)
@@ -245,8 +242,8 @@ def tile_latentattentionblock_pa_kernel(tc, x, norm_w, expand_w, out_0, out_1, o
         for n in range(-STATISTICS_AHEAD, N_PRODUCTS):
             rnd, step = n // STEPS, n % STEPS
             run = n + RUNS_AHEAD
-            if 0 <= run - 1 < N_RUNS:
-                w_quantise(run - 1)
+            if completes_chunk(run - 1):
+                w_quantise((run - 1) // 2)
             if product_waiting is not None:
                 gate_and_store(product_waiting)
             if block_starting_at(n + STATISTICS_AHEAD) is not None:

from contextlib import ExitStack

import concourse.masks as masks
import concourse.mybir as mybir

F32 = mybir.dt.float32
BF16 = mybir.dt.bfloat16
U32 = mybir.dt.uint32
U8 = mybir.dt.uint8
FP8X4 = mybir.dt.float8_e4m3fn_x4
ACT = mybir.ActivationFunctionType
ALU = mybir.AluOpType

P = 128
PACK = 4
K = 1024
PASSES = K // (P * PACK)
WORDS = K // 2
ROWS = 1024
N_BLOCKS = ROWS // P
HEAD = 128
QK = 2 * HEAD
E = 2048
CHUNK = 512
N_PAIRS = E // CHUNK
PRE, LIN = 0, 1
QK_CHUNK = 2 * N_PAIRS
RUN_ROW_BLOCKS = 2
N_RUNS = 2 * QK_CHUNK + 1
BN_STATS_MAX = 512
EPS = 1e-5
N_BANKS = 8

FIRST_BLOCKS = 4
STEPS = 4
N_PRODUCTS = N_BLOCKS * N_PAIRS
RUNS_AHEAD = 4
STATISTICS_AHEAD = 8
TRANSPOSE_AHEAD = 3
QUANTISE_AHEAD = 2

FLOPS = 2 * ROWS * K * (QK + 2 * E)


def tile_latentattentionblock_pa_kernel(tc, x, norm_w, expand_w, out_0, out_1, out_2):
    nc = tc.nc
    with ExitStack() as ctx:
        resident = ctx.enter_context(tc.tile_pool(name="resident", bufs=1))
        per_block = ctx.enter_context(tc.tile_pool(name="per_block", bufs=FIRST_BLOCKS))
        grouped_tiles = ctx.enter_context(tc.tile_pool(name="grouped_tiles", bufs=2))
        gates = ctx.enter_context(tc.tile_pool(name="gates", bufs=N_BANKS // 2 + 1))
        results = ctx.enter_context(tc.tile_pool(name="results", bufs=12))
        banks = ctx.enter_context(tc.psum_pool(name="banks", bufs=N_BANKS))

        x_rows = x.rearrange("o (p i) w -> p (o i) w", i=N_BLOCKS)
        q_rows = out_0.rearrange("o (p i) d -> p (o i) d", i=N_BLOCKS)
        k_rows = out_1.rearrange("o (p i) d -> p (o i) d", i=N_BLOCKS)
        geglu_rows = out_2.rearrange("o (p i) d -> p (o i) d", i=N_BLOCKS)

        x_raw = resident.tile([P, N_BLOCKS, K], BF16, name="x_raw")
        w_raw = resident.tile([P, (QK + 2 * E) // P * K], BF16, name="w_raw")
        w_words = w_raw[:].bitcast(F32)
        x_codes = resident.tile([P, N_BLOCKS * PASSES * P], U32, name="x_codes", align_bytes=64)
        x_scales = resident.tile([P, N_BLOCKS * PASSES * P], U8, name="x_scales", align_bytes=64)
        w_codes = resident.tile([P, PASSES * (2 * E + QK)], U32, name="w_codes", align_bytes=64)
        w_scales = resident.tile([P, PASSES * (2 * E + QK)], U8, name="w_scales", align_bytes=64)
        qk_stage = resident.tile([P, 2, N_BLOCKS, HEAD], F32, name="qk_stage")
        identity = resident.tile([P, P], F32, name="identity")
        gain_rows = resident.tile([P, 2 * P], BF16, name="gain_rows")
        gain = resident.tile([P, PASSES * PACK], F32, name="gain")
        minus_half = resident.tile([P, 1], F32, name="minus_half")
        warm = resident.tile([P, 1], F32, name="warm")

        def load_x(first, count):
            blocks = slice(first, first + count)
            nc.sync.dma_start(out=x_raw[:, blocks, :], in_=x_rows[:, blocks, :])

        def chunk_width(chunk):
            return QK if chunk == QK_CHUNK else CHUNK

        def chunk_row_block(chunk):
            if chunk == QK_CHUNK:
                return 0
            lin_first = (QK + chunk // 2 * CHUNK) // P
            return lin_first if chunk % 2 == LIN else lin_first + E // P

        def load_chunk(chunk, pieces):
            count = chunk_width(chunk) // P // pieces
            for piece in range(pieces):
                first = chunk_row_block(chunk) + piece * count
                nc.sync.dma_start(
                    out=w_raw[:, first * K : (first + count) * K].rearrange("p (i k) -> p i k", k=K),
                    in_=expand_w[first * P : (first + count) * P, :].rearrange("(i p) k -> p i k", p=P),
                )

        normalised = {}
        x_grouped = {}

        def x_normalise(b):
            stats = per_block.tile([P, K // BN_STATS_MAX, 6], F32, name="stats", tag="stats")
            for h in range(K // BN_STATS_MAX):
                nc.vector.bn_stats(out=stats[:, h, :], in_=x_raw[:, b, h * BN_STATS_MAX : (h + 1) * BN_STATS_MAX])
            moments = per_block.tile([P, 3], F32, name="moments", tag="moments")
            nc.vector.bn_aggr(out=moments[:, 0:2], in_=stats[:].rearrange("p h c -> p (h c)"))
            nc.vector.tensor_scalar_add(out=moments[:, 2:3], in0=moments[:, 1:2], scalar1=EPS)
            scale_bias = per_block.tile([P, 2], F32, name="scale_bias", tag="scale_bias")
            nc.gpsimd.tensor_tensor(out=scale_bias[:, 0:1], in0=moments[:, 2:3], in1=minus_half[:], op=ALU.pow)
            nc.gpsimd.tensor_scalar(
                out=scale_bias[:, 1:2],
                in0=moments[:, 0:1],
                scalar1=scale_bias[:, 0:1],
                scalar2=-1.0,
                op0=ALU.mult,
                op1=ALU.mult,
            )
            y = per_block.tile([P, K], F32, name="y", tag="y")
            nc.gpsimd.tensor_scalar(
                out=y[:].rearrange("p (a e q) -> p a e q", e=2, q=P),
                in0=x_raw[:, b, :].rearrange("p (a q e) -> p a e q", e=2, q=P),
                scalar1=scale_bias[:, 0:1],
                scalar2=scale_bias[:, 1:2],
                op0=ALU.mult,
                op1=ALU.add,
            )
            normalised[b] = y

        def spread_gain():
            gain_bank = banks.tile([P, P], F32, name="gain_bank", tag="bank")
            nc.tensor.transpose(gain_bank[:], gain_rows[:].bitcast(F32), identity[:])
            nc.vector.tensor_copy(out=gain[:], in_=gain_bank[:, 0 : PASSES * 2].bitcast(BF16))

        def x_transpose(b):
            y = normalised[b]
            grouped = grouped_tiles.tile([P, PASSES * P * PACK], BF16, name="x_grouped", tag="x", align_bytes=64)
            for g in range(PASSES):
                bank = banks.tile([P, PACK * P], F32, name="x_bank", tag="bank")
                for t in range(PACK):
                    column = (g * PACK + t) * P
                    nc.tensor.transpose(bank[:, t * P : (t + 1) * P], y[:, column : column + P], identity[:])
                nc.vector.tensor_tensor(
                    out=grouped[:, g * P * PACK : (g + 1) * P * PACK].rearrange("p (r t) -> p r t", t=PACK),
                    in0=bank[:].rearrange("p (t r) -> p r t", t=PACK),
                    in1=gain[:, g * PACK : (g + 1) * PACK].unsqueeze(1).to_broadcast([P, P, PACK]),
                    op=ALU.mult,
                )
            x_grouped[b] = grouped

        def x_quantise(b):
            columns = slice(b * PASSES * P, (b + 1) * PASSES * P)
            nc.vector.quantize_mx(
                out=x_codes[:, columns].bitcast(FP8X4), scales=x_scales[:, columns], in_=x_grouped[b][:]
            )

        w_grouped = {}

        def w_transpose(run):
            chunk = run // 2
            if run % 2 == 0:
                w_grouped[chunk] = grouped_tiles.tile(
                    [P, PASSES * chunk_width(chunk) * PACK], BF16, name="w_grouped", tag="w", align_bytes=64
                )
            grouped_words = w_grouped[chunk][:].bitcast(F32).rearrange("p (g n u) -> p g n u", g=PASSES, u=2)
            for i in range(RUN_ROW_BLOCKS):
                block = run % 2 * RUN_ROW_BLOCKS + i
                bank = banks.tile([P, PACK * P], F32, name="w_bank", tag="bank")
                for a in range(PACK):
                    column = (chunk_row_block(chunk) + block) * WORDS + a * P
                    nc.tensor.transpose(bank[:, a * P : (a + 1) * P], w_words[:, column : column + P], identity[:])
                nc.scalar.copy(
                    out=grouped_words[:, :, block * P : (block + 1) * P, :],
                    in_=bank[:].rearrange("p (g u r) -> p g r u", g=PASSES, u=2),
                )

        def completes_chunk(run):
            return 0 <= run < N_RUNS and (run % 2 == 1 or run // 2 == QK_CHUNK)

        def w_quantise(chunk):
            first = chunk * PASSES * CHUNK
            columns = slice(first, first + PASSES * chunk_width(chunk))
            nc.vector.quantize_mx(
                out=w_codes[:, columns].bitcast(FP8X4), scales=w_scales[:, columns], in_=w_grouped[chunk][:]
            )

        def multiply(acc, b, chunk):
            width = chunk_width(chunk)
            for g in range(PASSES):
                rows = slice((b * PASSES + g) * P, (b * PASSES + g + 1) * P)
                first = chunk * PASSES * CHUNK + g * width
                columns = slice(first, first + width)
                nc.tensor.matmul_mx(
                    out=acc,
                    lhsT=x_codes[:, rows].bitcast(FP8X4),
                    lhsT_scale=x_scales[:, rows],
                    rhs=w_codes[:, columns].bitcast(FP8X4),
                    rhs_scale=w_scales[:, columns],
                    start=(g == 0),
                    stop=(g == PASSES - 1),
                )

        def project_qk(b):
            acc = banks.tile([P, QK], F32, name="qk_acc", tag="bank")
            multiply(acc[:], b, QK_CHUNK)
            nc.scalar.copy(out=qk_stage[:, :, b, :], in_=acc[:].rearrange("p (h d) -> p h d", h=2))

        def multiply_pair(b, pair):
            pre = banks.tile([P, CHUNK], F32, name="pre", tag="bank")
            multiply(pre[:], b, 2 * pair + PRE)
            lin = banks.tile([P, CHUNK], F32, name="lin", tag="bank")
            multiply(lin[:], b, 2 * pair + LIN)
            gate = gates.tile([P, CHUNK], F32, name="gate", tag="gate")
            nc.scalar.activation(out=gate[:], in_=pre[:], func=ACT.Gelu)
            return b, pair, lin, gate

        def gate_and_store(product):
            b, pair, lin, gate = product
            geglu = results.tile([P, CHUNK], F32, name="geglu", tag="geglu")
            nc.vector.tensor_tensor(out=geglu[:], in0=lin[:], in1=gate[:], op=ALU.mult)
            nc.sync.dma_start(out=geglu_rows[:, b, pair * CHUNK : (pair + 1) * CHUNK], in_=geglu[:])

        nc.vector.memset(gain_rows[:].bitcast(F32), 0.0)
        nc.vector.memset(minus_half[:], -0.5)
        nc.scalar.activation(out=warm[:], in_=minus_half[:], func=ACT.Gelu)
        masks.make_identity(nc, identity[:])

        load_x(0, 1)
        nc.sync.dma_start(out=gain_rows[0:4, :], in_=norm_w.rearrange("(a c) -> a c", a=4))
        for b in range(1, FIRST_BLOCKS):
            load_x(b, 1)
        for chunk in range(QK_CHUNK + 1):
            load_chunk(chunk, 2 if chunk // 2 == 0 else 1)
            if chunk == 2 * 1 + LIN:
                load_x(FIRST_BLOCKS, N_BLOCKS - FIRST_BLOCKS)

        def block_starting_at(n):
            if 0 <= n < FIRST_BLOCKS:
                return n
            if n % STEPS == 0 and FIRST_BLOCKS <= n // STEPS < N_BLOCKS:
                return n // STEPS
            return None

        product_waiting = None
        for n in range(-STATISTICS_AHEAD, N_PRODUCTS):
            rnd, step = n // STEPS, n % STEPS
            run = n + RUNS_AHEAD
            if completes_chunk(run - 1):
                w_quantise((run - 1) // 2)
            if product_waiting is not None:
                gate_and_store(product_waiting)
            if block_starting_at(n + STATISTICS_AHEAD) is not None:
                x_normalise(block_starting_at(n + STATISTICS_AHEAD))
            if step == 0 and rnd >= FIRST_BLOCKS:
                project_qk(rnd - FIRST_BLOCKS)
                project_qk(rnd)
            if n == N_PRODUCTS - STEPS:
                nc.sync.dma_start(out=q_rows, in_=qk_stage[:, 0, :, :])
                nc.sync.dma_start(out=k_rows, in_=qk_stage[:, 1, :, :])
            if 0 <= run < N_RUNS:
                w_transpose(run)
            if n + TRANSPOSE_AHEAD == 0:
                spread_gain()
            if block_starting_at(n + TRANSPOSE_AHEAD) is not None:
                x_transpose(block_starting_at(n + TRANSPOSE_AHEAD))
            if block_starting_at(n + QUANTISE_AHEAD) is not None:
                x_quantise(block_starting_at(n + QUANTISE_AHEAD))
            if n >= 0:
                b, pair = (step, rnd) if rnd < FIRST_BLOCKS else (rnd, step)
                product_waiting = multiply_pair(b, pair)
        gate_and_store(product_waiting)
